import numpy as np
import ml_dtypes


def mxq(x, axis, fmt="e4m3"):
    dtype, down = {"e4m3": (ml_dtypes.float8_e4m3fn, 7), "e5m2": (ml_dtypes.float8_e5m2, 14)}[fmt]
    v = np.moveaxis(np.asarray(x, np.float32).astype(ml_dtypes.bfloat16).astype(np.float64), axis, -1)
    blocks = v.reshape(v.shape[:-1] + (-1, 32))
    amax = np.abs(blocks).max(-1, keepdims=True)
    byte = np.maximum(np.where(amax > 0, np.frexp(amax)[1] - 1 + 127, 0) - down, 1)
    scale = np.exp2(byte - 127.0)
    codes = (blocks / scale).astype(np.float32).astype(dtype).astype(np.float64)
    return np.moveaxis((codes * scale).reshape(v.shape), -1, axis)


WIDE = False


def mx_kscale(k):
    if not WIDE:
        return np.ones(k)
    levels = np.array([10, -10, 5, -5, 0])
    if k % 512:
        return np.exp2(np.random.permutation(np.resize(levels, k // 32))).repeat(32)
    a = np.empty((k // 512, 16))
    for p in range(k // 512):
        a[p, :8] = np.random.permutation(np.resize(levels, 8))
        for g in range(8):
            far = levels[np.abs(levels - a[p, g]) >= 10]
            a[p, g + 8] = far[np.random.randint(len(far))]
    return np.exp2(a.ravel()).repeat(32)


BF16 = ml_dtypes.bfloat16


def bf(x):
    return np.asarray(x, np.float32).astype(BF16)


def f64(x):
    return np.asarray(x).astype(np.float64)


M, N, H, D, P = 8192, 512, 2, 64, 1024
E = H * D


def rms_norm(x):
    return x * (1.0 / np.sqrt(np.mean(x * x, axis=-1, keepdims=True)))


def setup_inputs():
    s = mx_kscale(N)
    c = np.sqrt(np.mean(s * s))
    r = np.exp2(np.random.uniform(-1.0, 1.0, (M, 1)))
    return {"X": bf(np.random.standard_normal((M, N)) * r * s),
            "W_q": bf(np.random.standard_normal((N, E)) * 2.0 / np.sqrt(N) / s[:, None] * c),
            "W_k": bf(np.random.standard_normal((N, E)) * 0.5 / np.sqrt(N) / s[:, None] * c),
            "W_v": bf(np.random.standard_normal((N, E)) * 1.0 / np.sqrt(N) / s[:, None] * c)}


def reference(X, W_q, W_k, W_v):
    xq = mxq(rms_norm(f64(X)), 1, "e4m3")
    q = (xq @ mxq(f64(W_q), 0, "e4m3")).reshape(M, H, D)
    k = (xq @ mxq(f64(W_k), 0, "e4m3")).reshape(M, H, D)
    v = (xq @ mxq(f64(W_v), 0, "e4m3")).reshape(M, H, D)
    qn = rms_norm(q)
    kn = rms_norm(k)
    return qn, kn.transpose(1, 0, 2), v.transpose(1, 0, 2)

@@ -1,0 +1,221 @@
+from contextlib import ExitStack
+
+import concourse.mybir as mybir
+from concourse.masks import make_identity
+
+BF16 = mybir.dt.bfloat16
+F32 = mybir.dt.float32
+U32 = mybir.dt.uint32
+U8 = mybir.dt.uint8
+FP8X4 = mybir.dt.float8_e4m3fn_x4
+ACT = mybir.ActivationFunctionType
+ALU = mybir.AluOpType
+
+P = 128
+ROWS = 8192
+FEATURES = 512
+HEADS = 2
+HEAD_DIM = 64
+WIDTH = HEADS * HEAD_DIM
+TILES = ROWS // P
+GROUP = 4
+GROUPS = TILES // GROUP
+PAIR = 2
+
+FLOPS = 2 * ROWS * FEATURES * 3 * WIDTH
+
+
+def tile_flashinfer_normqknorm_pa_t_kernel(tc, X, W_q, W_k, W_v, out_0, out_1, out_2):
+    nc = tc.nc
+    x_rows = X.rearrange("(p t) k -> p t k", t=TILES)
+    q_rows = out_0.rearrange("(p t) h d -> p t (h d)", t=TILES)
+    k_rows = out_1.rearrange("h (p t) d -> p h t d", t=TILES)
+    v_rows = out_2.rearrange("h (p t) d -> p h t d", t=TILES)
+
+    with ExitStack() as ctx:
+        const = ctx.enter_context(tc.tile_pool(name="const", bufs=1))
+        xin = ctx.enter_context(tc.tile_pool(name="xin", bufs=GROUPS))
+        work = ctx.enter_context(tc.tile_pool(name="work", bufs=2))
+        small = ctx.enter_context(tc.tile_pool(name="small", bufs=3))
+        outs = ctx.enter_context(tc.tile_pool(name="outs", bufs=GROUPS))
+        psum = ctx.enter_context(tc.psum_pool(name="psum", bufs=2))
+        ctx.enter_context(tc.manual_schedule())
+
+        one = const.tile([P, 1], F32)
+        nc.vector.memset(one[:], 1.0)
+        root_of_one = const.tile([P, 1], F32)
+        nc.scalar.activation(out=root_of_one[:], in_=one[:], func=ACT.Sqrt)
+
+        ident = const.tile([P, P], F32)
+        make_identity(nc, ident[:])
+
+        x_sb, sum_sq, rms, inv_rms, xn, xt, grouped = {}, {}, {}, {}, {}, {}, {}
+        x_codes, x_scales, acc, moments, mean_sq, head_ms, head_rms, head_inv = {}, {}, {}, {}, {}, {}, {}, {}
+
+        def load(g):
+            x_sb[g] = xin.tile([P, GROUP, FEATURES], BF16, name="x_sb")
+            nc.sync.dma_start(out=x_sb[g][:], in_=x_rows[:, g * GROUP : (g + 1) * GROUP, :])
+
+        load(0)
+        w_raw = const.tile([P, 3, 4, WIDTH], BF16)
+        for w, weight in enumerate((W_q, W_k, W_v)):
+            nc.sync.dma_start(
+                out=w_raw[:, w, :, :],
+                in_=weight.rearrange("(p t) n -> p t n", t=4),
+            )
+        for g in range(1, GROUPS):
+            load(g)
+        w_grouped = const.tile([P, 3, WIDTH, 4], BF16, align_bytes=64)
+        nc.vector.tensor_copy(out=w_grouped[:], in_=w_raw[:].rearrange("p w t n -> p w n t"))
+        w_codes = const.tile([P, 3, WIDTH], U32, align_bytes=64)
+        w_scales = const.tile([P, 3, WIDTH], U8, align_bytes=64)
+        for w in range(3):
+            nc.vector.quantize_mx(
+                out=w_codes[:, w, :].bitcast(FP8X4),
+                scales=w_scales[:, w, :],
+                in_=w_grouped[:, w, :, :].rearrange("p n t -> p (n t)"),
+            )
+
+        def row_squares(g):
+            squares = work.tile([P, GROUP, FEATURES], BF16, name="squares")
+            sum_sq[g] = small.tile([P, GROUP], F32, name="sum_sq")
+            for j in range(GROUP):
+                nc.scalar.activation(
+                    out=squares[:, j, :], in_=x_sb[g][:, j, :], func=ACT.Square,
+                    accum_out=sum_sq[g][:, j : j + 1],
+                )
+
+        def row_root(g):
+            rms[g] = small.tile([P, GROUP], F32, name="rms")
+            nc.scalar.activation(out=rms[g][:], in_=sum_sq[g][:], func=ACT.Sqrt, scale=1.0 / FEATURES)
+
+        def invert_row_rms(g):
+            inv_rms[g] = small.tile([P, GROUP], F32, name="inv_rms")
+            nc.vector.reciprocal(out=inv_rms[g][:], in_=rms[g][:])
+
+        def normalise(g):
+            xn[g] = work.tile([P, GROUP, FEATURES], BF16, name="xn")
+            for j in range(GROUP):
+                nc.vector.tensor_scalar_mul(
+                    out=xn[g][:, j, :], in0=x_sb[g][:, j, :], scalar1=inv_rms[g][:, j : j + 1]
+                )
+
+        def transpose(g):
+            xt[g] = []
+            for j0 in range(0, GROUP, PAIR):
+                bank = psum.tile([P, PAIR, 2, P], F32, name="xt")
+                for jj in range(PAIR):
+                    words = xn[g][:, j0 + jj, :].bitcast(F32)
+                    for u in range(2):
+                        nc.tensor.transpose(bank[:, jj, u, :], words[:, u : 2 * P : 2], ident[:])
+                xt[g].append(bank)
+
+        def regroup(g):
+            grouped[g] = work.tile([P, GROUP, P, 4], BF16, name="grouped", align_bytes=64)
+            for b, bank in enumerate(xt[g]):
+                nc.scalar.copy(
+                    out=grouped[g][:, b * PAIR : (b + 1) * PAIR, :, :].bitcast(F32),
+                    in_=bank[:].rearrange("p j u r -> p j r u"),
+                )
+
+        def quantise(g):
+            x_codes[g] = work.tile([P, GROUP, P], U32, name="x_codes", align_bytes=64)
+            x_scales[g] = work.tile([P, GROUP, P], U8, name="x_scales", align_bytes=64)
+            nc.vector.quantize_mx(
+                out=x_codes[g][:].rearrange("p j r -> p (j r)").bitcast(FP8X4),
+                scales=x_scales[g][:].rearrange("p j r -> p (j r)"),
+                in_=grouped[g][:].rearrange("p j r t -> p (j r t)"),
+            )
+
+        def project(g):
+            acc[g] = []
+            for w, (name, bufs) in enumerate((("acc_q", 2), ("acc_k", 3), ("acc_v", 1))):
+                bank = psum.tile([P, GROUP, HEADS, HEAD_DIM], F32, name=name, bufs=bufs)
+                for j in range(GROUP):
+                    nc.tensor.matmul_mx(
+                        out=bank[:, j, :, :].rearrange("p h d -> p (h d)"),
+                        lhsT=x_codes[g][:, j, :].bitcast(FP8X4),
+                        lhsT_scale=x_scales[g][:, j, :],
+                        rhs=w_codes[:, w, :].bitcast(FP8X4),
+                        rhs_scale=w_scales[:, w, :],
+                        start=True,
+                        stop=True,
+                    )
+                acc[g].append(bank)
+
+        def head_moments(g):
+            moments[g] = small.tile([P, 2, GROUP, HEADS, 3], F32, name="moments")
+            for a in range(2):
+                for j in range(GROUP):
+                    nc.vector.bn_stats(
+                        out=moments[g][:, a, j, :, :].rearrange("p h s -> p (h s)"),
+                        in_=acc[g][a][:, j, :, :].rearrange("p h d -> p d h"),
+                    )
+
+        def square_head_means(g):
+            mean = moments[g][:, :, :, :, 1]
+            mean_sq[g] = small.tile([P, 2, GROUP, HEADS], F32, name="mean_sq")
+            nc.vector.tensor_tensor(out=mean_sq[g][:], in0=mean, in1=mean, op=ALU.mult)
+
+        def head_mean_squares(g):
+            head_ms[g] = small.tile([P, 2, GROUP, HEADS], F32, name="head_ms")
+            nc.vector.scalar_tensor_tensor(
+                out=head_ms[g][:], in0=moments[g][:, :, :, :, 2], scalar=1.0 / HEAD_DIM,
+                in1=mean_sq[g][:], op0=ALU.mult, op1=ALU.add,
+            )
+
+        def head_root(g):
+            head_rms[g] = small.tile([P, 2, GROUP, HEADS], F32, name="head_rms")
+            nc.scalar.activation(out=head_rms[g][:], in_=head_ms[g][:], func=ACT.Sqrt)
+
+        def invert_head_rms(g):
+            head_inv[g] = small.tile([P, 2, GROUP, HEADS], F32, name="head_inv")
+            nc.vector.reciprocal(out=head_inv[g][:], in_=head_rms[g][:])
+
+        def store_q(g):
+            q_sb = outs.tile([P, GROUP, HEADS, HEAD_DIM], F32, name="q_sb")
+            nc.vector.tensor_tensor(
+                out=q_sb[:], in0=acc[g][0][:],
+                in1=head_inv[g][:, 0].unsqueeze(3).to_broadcast([P, GROUP, HEADS, HEAD_DIM]),
+                op=ALU.mult,
+            )
+            nc.sync.dma_start(
+                out=q_rows[:, g * GROUP : (g + 1) * GROUP, :],
+                in_=q_sb[:].rearrange("p j h d -> p j (h d)"),
+            )
+
+        def store_k(g):
+            k_sb = outs.tile([P, HEADS, GROUP, HEAD_DIM], F32, name="k_sb")
+            nc.vector.tensor_tensor(
+                out=k_sb[:].rearrange("p h j d -> p j h d"), in0=acc[g][1][:],
+                in1=head_inv[g][:, 1].unsqueeze(3).to_broadcast([P, GROUP, HEADS, HEAD_DIM]),
+                op=ALU.mult,
+            )
+            nc.sync.dma_start(out=k_rows[:, :, g * GROUP : (g + 1) * GROUP, :], in_=k_sb[:])
+
+        def store_v(g):
+            v_sb = outs.tile([P, HEADS, GROUP, HEAD_DIM], F32, name="v_sb")
+            nc.vector.tensor_copy(out=v_sb[:].rearrange("p h j d -> p j h d"), in_=acc[g][2][:])
+            nc.sync.dma_start(out=v_rows[:, :, g * GROUP : (g + 1) * GROUP, :], in_=v_sb[:])
+
+        def run(stage, g):
+            if 0 <= g < GROUPS:
+                stage(g)
+
+        for i in range(-2, GROUPS + 2):
+            run(row_squares, i + 2)
+            run(head_moments, i - 1)
+            run(normalise, i + 1)
+            run(transpose, i + 1)
+            run(square_head_means, i - 1)
+            run(store_v, i - 1)
+            run(head_mean_squares, i - 1)
+            run(quantise, i)
+            run(project, i)
+            run(head_root, i - 1)
+            run(row_root, i + 2)
+            run(invert_head_rms, i - 1)
+            run(invert_row_rms, i + 2)
+            run(store_k, i - 2)
+            run(store_q, i - 1)
+            run(regroup, i + 1)

@@ -18,11 +18,19 @@ HEADS = 2
 HEAD_DIM = 64
 WIDTH = HEADS * HEAD_DIM
 TILES = ROWS // P
-GROUP = 4
-GROUPS = TILES // GROUP
 PAIR = 2
+FULL = 4
+SIZES = (PAIR, PAIR) + (FULL,) * 14 + (PAIR, PAIR)
+STARTS = tuple(sum(SIZES[:g]) for g in range(len(SIZES)))
+GROUPS = len(SIZES)
 
 FLOPS = 2 * ROWS * FEATURES * 3 * WIDTH
+
+
+def vector_tiles(g):
+    if g < 3:
+        return SIZES[g] // 2
+    return 1 if g % 2 == 0 and SIZES[g] == FULL else 0
 
 
 def tile_flashinfer_normqknorm_pa_t_kernel(tc, X, W_q, W_k, W_v, out_0, out_1, out_2):
@@ -36,73 +44,82 @@ def tile_flashinfer_normqknorm_pa_t_kernel(tc, X, W_q, W_k, W_v, out_0, out_1, o
         const = ctx.enter_context(tc.tile_pool(name="const", bufs=1))
         xin = ctx.enter_context(tc.tile_pool(name="xin", bufs=GROUPS))
         work = ctx.enter_context(tc.tile_pool(name="work", bufs=2))
-        small = ctx.enter_context(tc.tile_pool(name="small", bufs=3))
-        outs = ctx.enter_context(tc.tile_pool(name="outs", bufs=GROUPS))
+        stats = ctx.enter_context(tc.tile_pool(name="stats", bufs=GROUPS))
+        small = ctx.enter_context(tc.tile_pool(name="small", bufs=4))
+        outs = ctx.enter_context(tc.tile_pool(name="outs", bufs=12))
         psum = ctx.enter_context(tc.psum_pool(name="psum", bufs=2))
         ctx.enter_context(tc.manual_schedule())
 
         one = const.tile([P, 1], F32)
         nc.vector.memset(one[:], 1.0)
         root_of_one = const.tile([P, 1], F32)
-        nc.scalar.activation(out=root_of_one[:], in_=one[:], func=ACT.Sqrt)
+        nc.scalar.activation(out=root_of_one[:], in_=one[:], func=ACT.Abs_reciprocal_sqrt)
 
         ident = const.tile([P, P], F32)
         make_identity(nc, ident[:])
 
-        x_sb, sum_sq, rms, inv_rms, xn, xt, grouped = {}, {}, {}, {}, {}, {}, {}
-        x_codes, x_scales, acc, moments, mean_sq, head_ms, head_rms, head_inv = {}, {}, {}, {}, {}, {}, {}, {}
+        x_sb, sum_sq, inv_rms, xn, xt, grouped = {}, {}, {}, {}, {}, {}
+        x_codes, x_scales, acc, moments, mean_sq, head_ms, head_inv = {}, {}, {}, {}, {}, {}, {}
 
         def load(g):
-            x_sb[g] = xin.tile([P, GROUP, FEATURES], BF16, name="x_sb")
-            nc.sync.dma_start(out=x_sb[g][:], in_=x_rows[:, g * GROUP : (g + 1) * GROUP, :])
+            sum_sq[g] = stats.tile([P, SIZES[g]], F32, name="sum_sq")
+            x_sb[g] = xin.tile([P, SIZES[g], FEATURES], BF16, name="x_sb")
+            nc.sync.dma_start(out=x_sb[g][:], in_=x_rows[:, STARTS[g] : STARTS[g] + SIZES[g], :])
 
         load(0)
+        load(1)
         w_raw = const.tile([P, 3, 4, WIDTH], BF16)
         for w, weight in enumerate((W_q, W_k, W_v)):
-            nc.sync.dma_start(
-                out=w_raw[:, w, :, :],
-                in_=weight.rearrange("(p t) n -> p t n", t=4),
-            )
-        for g in range(1, GROUPS):
+            nc.sync.dma_start(out=w_raw[:, w, :, :], in_=weight.rearrange("(p t) n -> p t n", t=4))
+        for g in range(2, GROUPS):
             load(g)
-        w_grouped = const.tile([P, 3, WIDTH, 4], BF16, align_bytes=64)
-        nc.vector.tensor_copy(out=w_grouped[:], in_=w_raw[:].rearrange("p w t n -> p w n t"))
+
         w_codes = const.tile([P, 3, WIDTH], U32, align_bytes=64)
         w_scales = const.tile([P, 3, WIDTH], U8, align_bytes=64)
-        for w in range(3):
-            nc.vector.quantize_mx(
-                out=w_codes[:, w, :].bitcast(FP8X4),
-                scales=w_scales[:, w, :],
-                in_=w_grouped[:, w, :, :].rearrange("p n t -> p (n t)"),
-            )
 
-        def row_squares(g):
-            squares = work.tile([P, GROUP, FEATURES], BF16, name="squares")
-            sum_sq[g] = small.tile([P, GROUP], F32, name="sum_sq")
-            for j in range(GROUP):
+        def quantise_weights():
+            w_grouped = const.tile([P, 3, WIDTH, 4], BF16, name="w_grouped", align_bytes=64)
+            nc.vector.tensor_copy(out=w_grouped[:], in_=w_raw[:].rearrange("p w t n -> p w n t"))
+            for w in range(3):
+                nc.vector.quantize_mx(
+                    out=w_codes[:, w, :].bitcast(FP8X4),
+                    scales=w_scales[:, w, :],
+                    in_=w_grouped[:, w, :, :].rearrange("p n t -> p (n t)"),
+                )
+
+        def row_squares_on_vector(g):
+            for j in range(vector_tiles(g)):
+                squares = work.tile([P, FEATURES], BF16, name="squares_v")
+                nc.vector.scalar_tensor_tensor(
+                    out=squares[:], in0=x_sb[g][:, j, :], scalar=1.0, in1=x_sb[g][:, j, :],
+                    op0=ALU.mult, op1=ALU.mult, accum_out=sum_sq[g][:, j : j + 1],
+                )
+
+        def row_squares(g, part):
+            middle = (vector_tiles(g) + SIZES[g]) // 2
+            for j in range(vector_tiles(g), middle) if part == 0 else range(middle, SIZES[g]):
+                squares = work.tile([P, FEATURES], BF16, name="squares")
                 nc.scalar.activation(
-                    out=squares[:, j, :], in_=x_sb[g][:, j, :], func=ACT.Square,
+                    out=squares[:], in_=x_sb[g][:, j, :], func=ACT.Square,
                     accum_out=sum_sq[g][:, j : j + 1],
                 )
 
-        def row_root(g):
-            rms[g] = small.tile([P, GROUP], F32, name="rms")
-            nc.scalar.activation(out=rms[g][:], in_=sum_sq[g][:], func=ACT.Sqrt, scale=1.0 / FEATURES)
-
         def invert_row_rms(g):
-            inv_rms[g] = small.tile([P, GROUP], F32, name="inv_rms")
-            nc.vector.reciprocal(out=inv_rms[g][:], in_=rms[g][:])
+            inv_rms[g] = small.tile([P, SIZES[g]], F32, name="inv_rms")
+            nc.scalar.activation(
+                out=inv_rms[g][:], in_=sum_sq[g][:], func=ACT.Abs_reciprocal_sqrt, scale=1.0 / FEATURES
+            )
 
         def normalise(g):
-            xn[g] = work.tile([P, GROUP, FEATURES], BF16, name="xn")
-            for j in range(GROUP):
+            xn[g] = work.tile([P, SIZES[g], FEATURES], BF16, name="xn")
+            for j in range(SIZES[g]):
                 nc.vector.tensor_scalar_mul(
                     out=xn[g][:, j, :], in0=x_sb[g][:, j, :], scalar1=inv_rms[g][:, j : j + 1]
                 )
 
         def transpose(g):
             xt[g] = []
-            for j0 in range(0, GROUP, PAIR):
+            for j0 in range(0, SIZES[g], PAIR):
                 bank = psum.tile([P, PAIR, 2, P], F32, name="xt")
                 for jj in range(PAIR):
                     words = xn[g][:, j0 + jj, :].bitcast(F32)
@@ -111,7 +128,7 @@ def tile_flashinfer_normqknorm_pa_t_kernel(tc, X, W_q, W_k, W_v, out_0, out_1, o
                 xt[g].append(bank)
 
         def regroup(g):
-            grouped[g] = work.tile([P, GROUP, P, 4], BF16, name="grouped", align_bytes=64)
+            grouped[g] = work.tile([P, SIZES[g], P, 4], BF16, name="grouped", align_bytes=64)
             for b, bank in enumerate(xt[g]):
                 nc.scalar.copy(
                     out=grouped[g][:, b * PAIR : (b + 1) * PAIR, :, :].bitcast(F32),
@@ -119,8 +136,8 @@ def tile_flashinfer_normqknorm_pa_t_kernel(tc, X, W_q, W_k, W_v, out_0, out_1, o
                 )
 
         def quantise(g):
-            x_codes[g] = work.tile([P, GROUP, P], U32, name="x_codes", align_bytes=64)
-            x_scales[g] = work.tile([P, GROUP, P], U8, name="x_scales", align_bytes=64)
+            x_codes[g] = work.tile([P, SIZES[g], P], U32, name="x_codes", align_bytes=64)
+            x_scales[g] = work.tile([P, SIZES[g], P], U8, name="x_scales", align_bytes=64)
             nc.vector.quantize_mx(
                 out=x_codes[g][:].rearrange("p j r -> p (j r)").bitcast(FP8X4),
                 scales=x_scales[g][:].rearrange("p j r -> p (j r)"),
@@ -130,8 +147,8 @@ def tile_flashinfer_normqknorm_pa_t_kernel(tc, X, W_q, W_k, W_v, out_0, out_1, o
         def project(g):
             acc[g] = []
             for w, (name, bufs) in enumerate((("acc_q", 2), ("acc_k", 3), ("acc_v", 1))):
-                bank = psum.tile([P, GROUP, HEADS, HEAD_DIM], F32, name=name, bufs=bufs)
-                for j in range(GROUP):
+                bank = psum.tile([P, SIZES[g], HEADS, HEAD_DIM], F32, name=name, bufs=bufs)
+                for j in range(SIZES[g]):
                     nc.tensor.matmul_mx(
                         out=bank[:, j, :, :].rearrange("p h d -> p (h d)"),
                         lhsT=x_codes[g][:, j, :].bitcast(FP8X4),
@@ -144,9 +161,9 @@ def tile_flashinfer_normqknorm_pa_t_kernel(tc, X, W_q, W_k, W_v, out_0, out_1, o
                 acc[g].append(bank)
 
         def head_moments(g):
-            moments[g] = small.tile([P, 2, GROUP, HEADS, 3], F32, name="moments")
+            moments[g] = small.tile([P, 2, SIZES[g], HEADS, 3], F32, name="moments")
             for a in range(2):
-                for j in range(GROUP):
+                for j in range(SIZES[g]):
                     nc.vector.bn_stats(
                         out=moments[g][:, a, j, :, :].rearrange("p h s -> p (h s)"),
                         in_=acc[g][a][:, j, :, :].rearrange("p h d -> p d h"),
@@ -154,68 +171,67 @@ def tile_flashinfer_normqknorm_pa_t_kernel(tc, X, W_q, W_k, W_v, out_0, out_1, o
 
         def square_head_means(g):
             mean = moments[g][:, :, :, :, 1]
-            mean_sq[g] = small.tile([P, 2, GROUP, HEADS], F32, name="mean_sq")
+            mean_sq[g] = small.tile([P, 2, SIZES[g], HEADS], F32, name="mean_sq")
             nc.vector.tensor_tensor(out=mean_sq[g][:], in0=mean, in1=mean, op=ALU.mult)
 
         def head_mean_squares(g):
-            head_ms[g] = small.tile([P, 2, GROUP, HEADS], F32, name="head_ms")
+            head_ms[g] = small.tile([P, 2, SIZES[g], HEADS], F32, name="head_ms")
             nc.vector.scalar_tensor_tensor(
                 out=head_ms[g][:], in0=moments[g][:, :, :, :, 2], scalar=1.0 / HEAD_DIM,
                 in1=mean_sq[g][:], op0=ALU.mult, op1=ALU.add,
             )
 
-        def head_root(g):
-            head_rms[g] = small.tile([P, 2, GROUP, HEADS], F32, name="head_rms")
-            nc.scalar.activation(out=head_rms[g][:], in_=head_ms[g][:], func=ACT.Sqrt)
-
         def invert_head_rms(g):
-            head_inv[g] = small.tile([P, 2, GROUP, HEADS], F32, name="head_inv")
-            nc.vector.reciprocal(out=head_inv[g][:], in_=head_rms[g][:])
+            head_inv[g] = small.tile([P, 2, SIZES[g], HEADS], F32, name="head_inv")
+            nc.scalar.activation(out=head_inv[g][:], in_=head_ms[g][:], func=ACT.Abs_reciprocal_sqrt)
 
         def store_q(g):
-            q_sb = outs.tile([P, GROUP, HEADS, HEAD_DIM], F32, name="q_sb")
+            shape = [P, SIZES[g], HEADS, HEAD_DIM]
+            q_sb = outs.tile(shape, F32, name="q_sb")
             nc.vector.tensor_tensor(
                 out=q_sb[:], in0=acc[g][0][:],
-                in1=head_inv[g][:, 0].unsqueeze(3).to_broadcast([P, GROUP, HEADS, HEAD_DIM]),
+                in1=head_inv[g][:, 0].unsqueeze(3).to_broadcast(shape),
                 op=ALU.mult,
             )
             nc.sync.dma_start(
-                out=q_rows[:, g * GROUP : (g + 1) * GROUP, :],
+                out=q_rows[:, STARTS[g] : STARTS[g] + SIZES[g], :],
                 in_=q_sb[:].rearrange("p j h d -> p j (h d)"),
             )
 
         def store_k(g):
-            k_sb = outs.tile([P, HEADS, GROUP, HEAD_DIM], F32, name="k_sb")
+            k_sb = outs.tile([P, HEADS, SIZES[g], HEAD_DIM], F32, name="k_sb")
             nc.vector.tensor_tensor(
                 out=k_sb[:].rearrange("p h j d -> p j h d"), in0=acc[g][1][:],
-                in1=head_inv[g][:, 1].unsqueeze(3).to_broadcast([P, GROUP, HEADS, HEAD_DIM]),
+                in1=head_inv[g][:, 1].unsqueeze(3).to_broadcast([P, SIZES[g], HEADS, HEAD_DIM]),
                 op=ALU.mult,
             )
-            nc.sync.dma_start(out=k_rows[:, :, g * GROUP : (g + 1) * GROUP, :], in_=k_sb[:])
+            nc.sync.dma_start(out=k_rows[:, :, STARTS[g] : STARTS[g] + SIZES[g], :], in_=k_sb[:])
 
         def store_v(g):
-            v_sb = outs.tile([P, HEADS, GROUP, HEAD_DIM], F32, name="v_sb")
-            nc.vector.tensor_copy(out=v_sb[:].rearrange("p h j d -> p j h d"), in_=acc[g][2][:])
-            nc.sync.dma_start(out=v_rows[:, :, g * GROUP : (g + 1) * GROUP, :], in_=v_sb[:])
+            v_sb = outs.tile([P, HEADS, SIZES[g], HEAD_DIM], F32, name="v_sb")
+            nc.scalar.copy(out=v_sb[:].rearrange("p h j d -> p j h d"), in_=acc[g][2][:])
+            nc.sync.dma_start(out=v_rows[:, :, STARTS[g] : STARTS[g] + SIZES[g], :], in_=v_sb[:])
 
-        def run(stage, g):
+        def run(stage, g, *args):
             if 0 <= g < GROUPS:
-                stage(g)
+                stage(g, *args)
 
         for i in range(-2, GROUPS + 2):
-            run(row_squares, i + 2)
+            run(regroup, i + 0)
+            if i == -1:
+                quantise_weights()
             run(head_moments, i - 1)
+            run(square_head_means, i - 1)
             run(normalise, i + 1)
             run(transpose, i + 1)
-            run(square_head_means, i - 1)
-            run(store_v, i - 1)
             run(head_mean_squares, i - 1)
-            run(quantise, i)
-            run(project, i)
-            run(head_root, i - 1)
-            run(row_root, i + 2)
+            run(row_squares, i + 2, 0)
+            run(store_v, i - 1)
             run(invert_head_rms, i - 1)
-            run(invert_row_rms, i + 2)
+            run(quantise, i + 0)
+            run(project, i + 0)
+            run(row_squares, i + 2, 1)
+            run(row_squares_on_vector, i + 2)
             run(store_k, i - 2)
             run(store_q, i - 1)
-            run(regroup, i + 1)
+            run(invert_row_rms, i + 2)

@@ -28,7 +28,7 @@ FLOPS = 2 * ROWS * FEATURES * 3 * WIDTH
 
 
 def vector_tiles(g):
-    if g < 3:
+    if g < 4:
         return SIZES[g] // 2
     return 1 if g % 2 == 0 and SIZES[g] == FULL else 0
 
@@ -77,9 +77,14 @@ def tile_flashinfer_normqknorm_pa_t_kernel(tc, X, W_q, W_k, W_v, out_0, out_1, o
         w_codes = const.tile([P, 3, WIDTH], U32, align_bytes=64)
         w_scales = const.tile([P, 3, WIDTH], U8, align_bytes=64)
 
+        w_grouped = const.tile([P, 3, WIDTH, 4], BF16, align_bytes=64)
+        for w in range(3):
+            nc.gpsimd.tensor_scalar(
+                out=w_grouped[:, w, :, :], in0=w_raw[:, w, :, :].rearrange("p t n -> p n t"),
+                scalar1=1.0, scalar2=0.0, op0=ALU.mult, op1=ALU.add,
+            )
+
         def quantise_weights():
-            w_grouped = const.tile([P, 3, WIDTH, 4], BF16, name="w_grouped", align_bytes=64)
-            nc.vector.tensor_copy(out=w_grouped[:], in_=w_raw[:].rearrange("p w t n -> p w n t"))
             for w in range(3):
                 nc.vector.quantize_mx(
                     out=w_codes[:, w, :].bitcast(FP8X4),
@@ -114,17 +119,19 @@ def tile_flashinfer_normqknorm_pa_t_kernel(tc, X, W_q, W_k, W_v, out_0, out_1, o
             xn[g] = work.tile([P, SIZES[g], FEATURES], BF16, name="xn")
             for j in range(SIZES[g]):
                 nc.vector.tensor_scalar_mul(
-                    out=xn[g][:, j, :], in0=x_sb[g][:, j, :], scalar1=inv_rms[g][:, j : j + 1]
+                    out=xn[g][:, j, :].rearrange("p (u w e) -> p u w e", u=2, e=2),
+                    in0=x_sb[g][:, j, :].rearrange("p (w u e) -> p u w e", u=2, e=2),
+                    scalar1=inv_rms[g][:, j : j + 1],
                 )
 
         def transpose(g):
             xt[g] = []
             for j0 in range(0, SIZES[g], PAIR):
-                bank = psum.tile([P, PAIR, 2, P], F32, name="xt")
-                for jj in range(PAIR):
+                bank = psum.tile([P, min(PAIR, SIZES[g]), 2, P], F32, name="xt")
+                for jj in range(min(PAIR, SIZES[g])):
                     words = xn[g][:, j0 + jj, :].bitcast(F32)
                     for u in range(2):
-                        nc.tensor.transpose(bank[:, jj, u, :], words[:, u : 2 * P : 2], ident[:])
+                        nc.tensor.transpose(bank[:, jj, u, :], words[:, u * P : (u + 1) * P], ident[:])
                 xt[g].append(bank)
 
         def regroup(g):
@@ -218,8 +225,6 @@ def tile_flashinfer_normqknorm_pa_t_kernel(tc, X, W_q, W_k, W_v, out_0, out_1, o
 
         for i in range(-2, GROUPS + 2):
             run(regroup, i + 0)
-            if i == -1:
-                quantise_weights()
             run(head_moments, i - 1)
             run(square_head_means, i - 1)
             run(normalise, i + 1)
@@ -228,6 +233,8 @@ def tile_flashinfer_normqknorm_pa_t_kernel(tc, X, W_q, W_k, W_v, out_0, out_1, o
             run(row_squares, i + 2, 0)
             run(store_v, i - 1)
             run(invert_head_rms, i - 1)
+            if i == 0:
+                quantise_weights()
             run(quantise, i + 0)
             run(project, i + 0)
             run(row_squares, i + 2, 1)

@@ -115,9 +115,11 @@ def tile_flashinfer_normqknorm_pa_t_kernel(tc, X, W_q, W_k, W_v, out_0, out_1, o
                 out=inv_rms[g][:], in_=sum_sq[g][:], func=ACT.Abs_reciprocal_sqrt, scale=1.0 / FEATURES
             )
 
-        def normalise(g):
-            xn[g] = work.tile([P, SIZES[g], FEATURES], BF16, name="xn")
-            for j in range(SIZES[g]):
+        def normalise(g, part):
+            if part == 0:
+                xn[g] = work.tile([P, SIZES[g], FEATURES], BF16, name="xn")
+            last = SIZES[g] - 1
+            for j in range(last) if part == 0 else (last,):
                 nc.vector.tensor_scalar_mul(
                     out=xn[g][:, j, :].rearrange("p (u w e) -> p u w e", u=2, e=2),
                     in0=x_sb[g][:, j, :].rearrange("p (w u e) -> p u w e", u=2, e=2),
@@ -223,22 +225,23 @@ def tile_flashinfer_normqknorm_pa_t_kernel(tc, X, W_q, W_k, W_v, out_0, out_1, o
             if 0 <= g < GROUPS:
                 stage(g, *args)
 
-        for i in range(-2, GROUPS + 2):
-            run(regroup, i + 0)
-            run(head_moments, i - 1)
-            run(square_head_means, i - 1)
-            run(normalise, i + 1)
-            run(transpose, i + 1)
-            run(head_mean_squares, i - 1)
+        for i in range(-3, GROUPS + 2):
+            run(normalise, i + 1, 0)
             run(row_squares, i + 2, 0)
             run(store_v, i - 1)
+            run(head_moments, i - 1)
+            run(square_head_means, i - 1)
+            run(normalise, i + 1, 1)
+            run(transpose, i + 1)
+            run(head_mean_squares, i - 1)
+            run(row_squares, i + 2, 1)
             run(invert_head_rms, i - 1)
+            run(invert_row_rms, i + 2)
             if i == 0:
                 quantise_weights()
             run(quantise, i + 0)
             run(project, i + 0)
-            run(row_squares, i + 2, 1)
-            run(row_squares_on_vector, i + 2)
+            run(row_squares_on_vector, i + 3)
             run(store_k, i - 2)
             run(store_q, i - 1)
-            run(invert_row_rms, i + 2)
+            run(regroup, i + 1)

@@ -101,8 +101,8 @@ def tile_flashinfer_normqknorm_pa_t_kernel(tc, X, W_q, W_k, W_v, out_0, out_1, o
                 )
 
         def row_squares(g, part):
-            middle = (vector_tiles(g) + SIZES[g]) // 2
-            for j in range(vector_tiles(g), middle) if part == 0 else range(middle, SIZES[g]):
+            first, last = SIZES[g] - 2, SIZES[g] - 1
+            for j in (range(vector_tiles(g), first), range(max(first, vector_tiles(g)), last), (last,))[part]:
                 squares = work.tile([P, FEATURES], BF16, name="squares")
                 nc.scalar.activation(
                     out=squares[:], in_=x_sb[g][:, j, :], func=ACT.Square,
@@ -118,8 +118,8 @@ def tile_flashinfer_normqknorm_pa_t_kernel(tc, X, W_q, W_k, W_v, out_0, out_1, o
         def normalise(g, part):
             if part == 0:
                 xn[g] = work.tile([P, SIZES[g], FEATURES], BF16, name="xn")
-            last = SIZES[g] - 1
-            for j in range(last) if part == 0 else (last,):
+            middle = SIZES[g] // 2
+            for j in range(middle) if part == 0 else range(middle, SIZES[g]):
                 nc.vector.tensor_scalar_mul(
                     out=xn[g][:, j, :].rearrange("p (u w e) -> p u w e", u=2, e=2),
                     in0=x_sb[g][:, j, :].rearrange("p (w u e) -> p u w e", u=2, e=2),
@@ -136,9 +136,10 @@ def tile_flashinfer_normqknorm_pa_t_kernel(tc, X, W_q, W_k, W_v, out_0, out_1, o
                         nc.tensor.transpose(bank[:, jj, u, :], words[:, u * P : (u + 1) * P], ident[:])
                 xt[g].append(bank)
 
-        def regroup(g):
-            grouped[g] = work.tile([P, SIZES[g], P, 4], BF16, name="grouped", align_bytes=64)
-            for b, bank in enumerate(xt[g]):
+        def regroup(g, part):
+            if part == 0:
+                grouped[g] = work.tile([P, SIZES[g], P, 4], BF16, name="grouped", align_bytes=64)
+            for b, bank in list(enumerate(xt[g]))[part : part + 1]:
                 nc.scalar.copy(
                     out=grouped[g][:, b * PAIR : (b + 1) * PAIR, :, :].bitcast(F32),
                     in_=bank[:].rearrange("p j u r -> p j r u"),
@@ -226,17 +227,17 @@ def tile_flashinfer_normqknorm_pa_t_kernel(tc, X, W_q, W_k, W_v, out_0, out_1, o
                 stage(g, *args)
 
         for i in range(-3, GROUPS + 2):
-            run(normalise, i + 1, 0)
             run(row_squares, i + 2, 0)
             run(store_v, i - 1)
             run(head_moments, i - 1)
+            run(normalise, i + 1, 0)
             run(square_head_means, i - 1)
             run(normalise, i + 1, 1)
             run(transpose, i + 1)
             run(head_mean_squares, i - 1)
             run(row_squares, i + 2, 1)
             run(invert_head_rms, i - 1)
-            run(invert_row_rms, i + 2)
+            run(row_squares, i + 2, 2)
             if i == 0:
                 quantise_weights()
             run(quantise, i + 0)
@@ -244,4 +245,6 @@ def tile_flashinfer_normqknorm_pa_t_kernel(tc, X, W_q, W_k, W_v, out_0, out_1, o
             run(row_squares_on_vector, i + 3)
             run(store_k, i - 2)
             run(store_q, i - 1)
-            run(regroup, i + 1)
+            run(regroup, i + 1, 0)
+            run(invert_row_rms, i + 2)
+            run(regroup, i + 1, 1)

@@ -20,7 +20,7 @@ WIDTH = HEADS * HEAD_DIM
 TILES = ROWS // P
 PAIR = 2
 FULL = 4
-SIZES = (PAIR, PAIR) + (FULL,) * 14 + (PAIR, PAIR)
+SIZES = () + (FULL,) * 16 + ()
 STARTS = tuple(sum(SIZES[:g]) for g in range(len(SIZES)))
 GROUPS = len(SIZES)
 
@@ -28,7 +28,7 @@ FLOPS = 2 * ROWS * FEATURES * 3 * WIDTH
 
 
 def vector_tiles(g):
-    if g < 4:
+    if g < 2:
         return SIZES[g] // 2
     return 1 if g % 2 == 0 and SIZES[g] == FULL else 0
 
@@ -64,7 +64,11 @@ def tile_flashinfer_normqknorm_pa_t_kernel(tc, X, W_q, W_k, W_v, out_0, out_1, o
         def load(g):
             sum_sq[g] = stats.tile([P, SIZES[g]], F32, name="sum_sq")
             x_sb[g] = xin.tile([P, SIZES[g], FEATURES], BF16, name="x_sb")
-            nc.sync.dma_start(out=x_sb[g][:], in_=x_rows[:, STARTS[g] : STARTS[g] + SIZES[g], :])
+            for j in ((0, 2, 1, 3) if g == 0 else (None,)):
+                if j is None:
+                    nc.sync.dma_start(out=x_sb[g][:], in_=x_rows[:, STARTS[g] : STARTS[g] + SIZES[g], :])
+                else:
+                    nc.sync.dma_start(out=x_sb[g][:, j, :], in_=x_rows[:, j, :])
 
         load(0)
         load(1)
@@ -226,7 +230,7 @@ def tile_flashinfer_normqknorm_pa_t_kernel(tc, X, W_q, W_k, W_v, out_0, out_1, o
             if 0 <= g < GROUPS:
                 stage(g, *args)
 
-        for i in range(-3, GROUPS + 2):
+        for i in range(-2, GROUPS + 2):
             run(row_squares, i + 2, 0)
             run(store_v, i - 1)
             run(head_moments, i - 1)
@@ -242,7 +246,7 @@ def tile_flashinfer_normqknorm_pa_t_kernel(tc, X, W_q, W_k, W_v, out_0, out_1, o
                 quantise_weights()
             run(quantise, i + 0)
             run(project, i + 0)
-            run(row_squares_on_vector, i + 3)
+            run(row_squares_on_vector, i + 2)
             run(store_k, i - 2)
             run(store_q, i - 1)
             run(regroup, i + 1, 0)

@@ -24,6 +24,8 @@ SIZES = () + (FULL,) * 16 + ()
 STARTS = tuple(sum(SIZES[:g]) for g in range(len(SIZES)))
 GROUPS = len(SIZES)
 
+KEEP_BUSY = 4
+
 FLOPS = 2 * ROWS * FEATURES * 3 * WIDTH
 
 
@@ -135,6 +137,11 @@ def tile_flashinfer_normqknorm_pa_t_kernel(tc, X, W_q, W_k, W_v, out_0, out_1, o
             for j0 in range(0, SIZES[g], PAIR):
                 bank = psum.tile([P, min(PAIR, SIZES[g]), 2, P], F32, name="xt")
                 for jj in range(min(PAIR, SIZES[g])):
+                    if j0 + jj == 0:
+                        for d in range(KEEP_BUSY):
+                            nc.tensor.matmul(
+                                out=bank[:, jj, 0, :], lhsT=ident[:], rhs=ident[:], start=True, stop=True
+                            )
                     words = xn[g][:, j0 + jj, :].bitcast(F32)
                     for u in range(2):
                         nc.tensor.transpose(bank[:, jj, u, :], words[:, u * P : (u + 1) * P], ident[:])

@@ -46,9 +46,10 @@ def tile_flashinfer_normqknorm_pa_t_kernel(tc, X, W_q, W_k, W_v, out_0, out_1, o
         const = ctx.enter_context(tc.tile_pool(name="const", bufs=1))
         xin = ctx.enter_context(tc.tile_pool(name="xin", bufs=GROUPS))
         work = ctx.enter_context(tc.tile_pool(name="work", bufs=2))
+        junk = ctx.enter_context(tc.tile_pool(name="junk", bufs=2 * FULL))
         stats = ctx.enter_context(tc.tile_pool(name="stats", bufs=GROUPS))
         small = ctx.enter_context(tc.tile_pool(name="small", bufs=4))
-        outs = ctx.enter_context(tc.tile_pool(name="outs", bufs=12))
+        outs = ctx.enter_context(tc.tile_pool(name="outs", bufs=GROUPS))
         psum = ctx.enter_context(tc.psum_pool(name="psum", bufs=2))
         ctx.enter_context(tc.manual_schedule())
 
@@ -100,7 +101,7 @@ def tile_flashinfer_normqknorm_pa_t_kernel(tc, X, W_q, W_k, W_v, out_0, out_1, o
 
         def row_squares_on_vector(g):
             for j in range(vector_tiles(g)):
-                squares = work.tile([P, FEATURES], BF16, name="squares_v")
+                squares = junk.tile([P, FEATURES], BF16, name="squares_v")
                 nc.vector.scalar_tensor_tensor(
                     out=squares[:], in0=x_sb[g][:, j, :], scalar=1.0, in1=x_sb[g][:, j, :],
                     op0=ALU.mult, op1=ALU.mult, accum_out=sum_sq[g][:, j : j + 1],
@@ -109,7 +110,7 @@ def tile_flashinfer_normqknorm_pa_t_kernel(tc, X, W_q, W_k, W_v, out_0, out_1, o
         def row_squares(g, part):
             first, last = SIZES[g] - 2, SIZES[g] - 1
             for j in (range(vector_tiles(g), first), range(max(first, vector_tiles(g)), last), (last,))[part]:
-                squares = work.tile([P, FEATURES], BF16, name="squares")
+                squares = junk.tile([P, FEATURES], BF16, name="squares")
                 nc.scalar.activation(
                     out=squares[:], in_=x_sb[g][:, j, :], func=ACT.Square,
                     accum_out=sum_sq[g][:, j : j + 1],
@@ -183,7 +184,7 @@ def tile_flashinfer_normqknorm_pa_t_kernel(tc, X, W_q, W_k, W_v, out_0, out_1, o
 
         def head_moments(g):
             moments[g] = small.tile([P, 2, SIZES[g], HEADS, 3], F32, name="moments")
-            for a in range(2):
+            for a in (0, 1):
                 for j in range(SIZES[g]):
                     nc.vector.bn_stats(
                         out=moments[g][:, a, j, :, :].rearrange("p h s -> p (h s)"),
@@ -257,5 +258,5 @@ def tile_flashinfer_normqknorm_pa_t_kernel(tc, X, W_q, W_k, W_v, out_0, out_1, o
             run(store_k, i - 2)
             run(store_q, i - 1)
             run(regroup, i + 1, 0)
-            run(invert_row_rms, i + 2)
             run(regroup, i + 1, 1)
+            run(invert_row_rms, i + 2)

@@ -32,7 +32,7 @@ FLOPS = 2 * ROWS * FEATURES * 3 * WIDTH
 def vector_tiles(g):
     if g < 2:
         return SIZES[g] // 2
-    return 1 if g % 2 == 0 and SIZES[g] == FULL else 0
+    return 1 if g % 4 == 2 else 0
 
 
 def tile_flashinfer_normqknorm_pa_t_kernel(tc, X, W_q, W_k, W_v, out_0, out_1, out_2):
@@ -258,5 +258,5 @@ def tile_flashinfer_normqknorm_pa_t_kernel(tc, X, W_q, W_k, W_v, out_0, out_1, o
             run(store_k, i - 2)
             run(store_q, i - 1)
             run(regroup, i + 1, 0)
-            run(regroup, i + 1, 1)
             run(invert_row_rms, i + 2)
+            run(regroup, i + 1, 1)

from contextlib import ExitStack

import concourse.mybir as mybir
from concourse.masks import make_identity

BF16 = mybir.dt.bfloat16
F32 = mybir.dt.float32
U32 = mybir.dt.uint32
U8 = mybir.dt.uint8
FP8X4 = mybir.dt.float8_e4m3fn_x4
ACT = mybir.ActivationFunctionType
ALU = mybir.AluOpType

P = 128
ROWS = 8192
FEATURES = 512
HEADS = 2
HEAD_DIM = 64
WIDTH = HEADS * HEAD_DIM
TILES = ROWS // P
PAIR = 2
FULL = 4
SIZES = () + (FULL,) * 16 + ()
STARTS = tuple(sum(SIZES[:g]) for g in range(len(SIZES)))
GROUPS = len(SIZES)

KEEP_BUSY = 4

FLOPS = 2 * ROWS * FEATURES * 3 * WIDTH


def vector_tiles(g):
    if g < 2:
        return SIZES[g] // 2
    return 1 if g % 4 == 2 else 0


def tile_flashinfer_normqknorm_pa_t_kernel(tc, X, W_q, W_k, W_v, out_0, out_1, out_2):
    nc = tc.nc
    x_rows = X.rearrange("(p t) k -> p t k", t=TILES)
    q_rows = out_0.rearrange("(p t) h d -> p t (h d)", t=TILES)
    k_rows = out_1.rearrange("h (p t) d -> p h t d", t=TILES)
    v_rows = out_2.rearrange("h (p t) d -> p h t d", t=TILES)

    with ExitStack() as ctx:
        const = ctx.enter_context(tc.tile_pool(name="const", bufs=1))
        xin = ctx.enter_context(tc.tile_pool(name="xin", bufs=GROUPS))
        work = ctx.enter_context(tc.tile_pool(name="work", bufs=2))
        junk = ctx.enter_context(tc.tile_pool(name="junk", bufs=2 * FULL))
        stats = ctx.enter_context(tc.tile_pool(name="stats", bufs=GROUPS))
        small = ctx.enter_context(tc.tile_pool(name="small", bufs=4))
        outs = ctx.enter_context(tc.tile_pool(name="outs", bufs=GROUPS))
        psum = ctx.enter_context(tc.psum_pool(name="psum", bufs=2))
        ctx.enter_context(tc.manual_schedule())

        one = const.tile([P, 1], F32)
        nc.vector.memset(one[:], 1.0)
        root_of_one = const.tile([P, 1], F32)
        nc.scalar.activation(out=root_of_one[:], in_=one[:], func=ACT.Abs_reciprocal_sqrt)

        ident = const.tile([P, P], F32)
        make_identity(nc, ident[:])

        x_sb, sum_sq, inv_rms, xn, xt, grouped = {}, {}, {}, {}, {}, {}
        x_codes, x_scales, acc, moments, mean_sq, head_ms, head_inv = {}, {}, {}, {}, {}, {}, {}

        def load(g):
            sum_sq[g] = stats.tile([P, SIZES[g]], F32, name="sum_sq")
            x_sb[g] = xin.tile([P, SIZES[g], FEATURES], BF16, name="x_sb")
            for j in ((0, 2, 1, 3) if g == 0 else (None,)):
                if j is None:
                    nc.sync.dma_start(out=x_sb[g][:], in_=x_rows[:, STARTS[g] : STARTS[g] + SIZES[g], :])
                else:
                    nc.sync.dma_start(out=x_sb[g][:, j, :], in_=x_rows[:, j, :])

        load(0)
        load(1)
        w_raw = const.tile([P, 3, 4, WIDTH], BF16)
        for w, weight in enumerate((W_q, W_k, W_v)):
            nc.sync.dma_start(out=w_raw[:, w, :, :], in_=weight.rearrange("(p t) n -> p t n", t=4))
        for g in range(2, GROUPS):
            load(g)

        w_codes = const.tile([P, 3, WIDTH], U32, align_bytes=64)
        w_scales = const.tile([P, 3, WIDTH], U8, align_bytes=64)

        w_grouped = const.tile([P, 3, WIDTH, 4], BF16, align_bytes=64)
        for w in range(3):
            nc.gpsimd.tensor_scalar(
                out=w_grouped[:, w, :, :], in0=w_raw[:, w, :, :].rearrange("p t n -> p n t"),
                scalar1=1.0, scalar2=0.0, op0=ALU.mult, op1=ALU.add,
            )

        def quantise_weights():
            for w in range(3):
                nc.vector.quantize_mx(
                    out=w_codes[:, w, :].bitcast(FP8X4),
                    scales=w_scales[:, w, :],
                    in_=w_grouped[:, w, :, :].rearrange("p n t -> p (n t)"),
                )

        def row_squares_on_vector(g):
            for j in range(vector_tiles(g)):
                squares = junk.tile([P, FEATURES], BF16, name="squares_v")
                nc.vector.scalar_tensor_tensor(
                    out=squares[:], in0=x_sb[g][:, j, :], scalar=1.0, in1=x_sb[g][:, j, :],
                    op0=ALU.mult, op1=ALU.mult, accum_out=sum_sq[g][:, j : j + 1],
                )

        def row_squares(g, part):
            first, last = SIZES[g] - 2, SIZES[g] - 1
            for j in (range(vector_tiles(g), first), range(max(first, vector_tiles(g)), last), (last,))[part]:
                squares = junk.tile([P, FEATURES], BF16, name="squares")
                nc.scalar.activation(
                    out=squares[:], in_=x_sb[g][:, j, :], func=ACT.Square,
                    accum_out=sum_sq[g][:, j : j + 1],
                )

        def invert_row_rms(g):
            inv_rms[g] = small.tile([P, SIZES[g]], F32, name="inv_rms")
            nc.scalar.activation(
                out=inv_rms[g][:], in_=sum_sq[g][:], func=ACT.Abs_reciprocal_sqrt, scale=1.0 / FEATURES
            )

        def normalise(g, part):
            if part == 0:
                xn[g] = work.tile([P, SIZES[g], FEATURES], BF16, name="xn")
            middle = SIZES[g] // 2
            for j in range(middle) if part == 0 else range(middle, SIZES[g]):
                nc.vector.tensor_scalar_mul(
                    out=xn[g][:, j, :].rearrange("p (u w e) -> p u w e", u=2, e=2),
                    in0=x_sb[g][:, j, :].rearrange("p (w u e) -> p u w e", u=2, e=2),
                    scalar1=inv_rms[g][:, j : j + 1],
                )

        def transpose(g):
            xt[g] = []
            for j0 in range(0, SIZES[g], PAIR):
                bank = psum.tile([P, min(PAIR, SIZES[g]), 2, P], F32, name="xt")
                for jj in range(min(PAIR, SIZES[g])):
                    if j0 + jj == 0:
                        for d in range(KEEP_BUSY):
                            nc.tensor.matmul(
                                out=bank[:, jj, 0, :], lhsT=ident[:], rhs=ident[:], start=True, stop=True
                            )
                    words = xn[g][:, j0 + jj, :].bitcast(F32)
                    for u in range(2):
                        nc.tensor.transpose(bank[:, jj, u, :], words[:, u * P : (u + 1) * P], ident[:])
                xt[g].append(bank)

        def regroup(g, part):
            if part == 0:
                grouped[g] = work.tile([P, SIZES[g], P, 4], BF16, name="grouped", align_bytes=64)
            for b, bank in list(enumerate(xt[g]))[part : part + 1]:
                nc.scalar.copy(
                    out=grouped[g][:, b * PAIR : (b + 1) * PAIR, :, :].bitcast(F32),
                    in_=bank[:].rearrange("p j u r -> p j r u"),
                )

        def quantise(g):
            x_codes[g] = work.tile([P, SIZES[g], P], U32, name="x_codes", align_bytes=64)
            x_scales[g] = work.tile([P, SIZES[g], P], U8, name="x_scales", align_bytes=64)
            nc.vector.quantize_mx(
                out=x_codes[g][:].rearrange("p j r -> p (j r)").bitcast(FP8X4),
                scales=x_scales[g][:].rearrange("p j r -> p (j r)"),
                in_=grouped[g][:].rearrange("p j r t -> p (j r t)"),
            )

        def project(g):
            acc[g] = []
            for w, (name, bufs) in enumerate((("acc_q", 2), ("acc_k", 3), ("acc_v", 1))):
                bank = psum.tile([P, SIZES[g], HEADS, HEAD_DIM], F32, name=name, bufs=bufs)
                for j in range(SIZES[g]):
                    nc.tensor.matmul_mx(
                        out=bank[:, j, :, :].rearrange("p h d -> p (h d)"),
                        lhsT=x_codes[g][:, j, :].bitcast(FP8X4),
                        lhsT_scale=x_scales[g][:, j, :],
                        rhs=w_codes[:, w, :].bitcast(FP8X4),
                        rhs_scale=w_scales[:, w, :],
                        start=True,
                        stop=True,
                    )
                acc[g].append(bank)

        def head_moments(g):
            moments[g] = small.tile([P, 2, SIZES[g], HEADS, 3], F32, name="moments")
            for a in (0, 1):
                for j in range(SIZES[g]):
                    nc.vector.bn_stats(
                        out=moments[g][:, a, j, :, :].rearrange("p h s -> p (h s)"),
                        in_=acc[g][a][:, j, :, :].rearrange("p h d -> p d h"),
                    )

        def square_head_means(g):
            mean = moments[g][:, :, :, :, 1]
            mean_sq[g] = small.tile([P, 2, SIZES[g], HEADS], F32, name="mean_sq")
            nc.vector.tensor_tensor(out=mean_sq[g][:], in0=mean, in1=mean, op=ALU.mult)

        def head_mean_squares(g):
            head_ms[g] = small.tile([P, 2, SIZES[g], HEADS], F32, name="head_ms")
            nc.vector.scalar_tensor_tensor(
                out=head_ms[g][:], in0=moments[g][:, :, :, :, 2], scalar=1.0 / HEAD_DIM,
                in1=mean_sq[g][:], op0=ALU.mult, op1=ALU.add,
            )

        def invert_head_rms(g):
            head_inv[g] = small.tile([P, 2, SIZES[g], HEADS], F32, name="head_inv")
            nc.scalar.activation(out=head_inv[g][:], in_=head_ms[g][:], func=ACT.Abs_reciprocal_sqrt)

        def store_q(g):
            shape = [P, SIZES[g], HEADS, HEAD_DIM]
            q_sb = outs.tile(shape, F32, name="q_sb")
            nc.vector.tensor_tensor(
                out=q_sb[:], in0=acc[g][0][:],
                in1=head_inv[g][:, 0].unsqueeze(3).to_broadcast(shape),
                op=ALU.mult,
            )
            nc.sync.dma_start(
                out=q_rows[:, STARTS[g] : STARTS[g] + SIZES[g], :],
                in_=q_sb[:].rearrange("p j h d -> p j (h d)"),
            )

        def store_k(g):
            k_sb = outs.tile([P, HEADS, SIZES[g], HEAD_DIM], F32, name="k_sb")
            nc.vector.tensor_tensor(
                out=k_sb[:].rearrange("p h j d -> p j h d"), in0=acc[g][1][:],
                in1=head_inv[g][:, 1].unsqueeze(3).to_broadcast([P, SIZES[g], HEADS, HEAD_DIM]),
                op=ALU.mult,
            )
            nc.sync.dma_start(out=k_rows[:, :, STARTS[g] : STARTS[g] + SIZES[g], :], in_=k_sb[:])

        def store_v(g):
            v_sb = outs.tile([P, HEADS, SIZES[g], HEAD_DIM], F32, name="v_sb")
            nc.scalar.copy(out=v_sb[:].rearrange("p h j d -> p j h d"), in_=acc[g][2][:])
            nc.sync.dma_start(out=v_rows[:, :, STARTS[g] : STARTS[g] + SIZES[g], :], in_=v_sb[:])

        def run(stage, g, *args):
            if 0 <= g < GROUPS:
                stage(g, *args)

        for i in range(-2, GROUPS + 2):
            run(row_squares, i + 2, 0)
            run(store_v, i - 1)
            run(head_moments, i - 1)
            run(normalise, i + 1, 0)
            run(square_head_means, i - 1)
            run(normalise, i + 1, 1)
            run(transpose, i + 1)
            run(head_mean_squares, i - 1)
            run(row_squares, i + 2, 1)
            run(invert_head_rms, i - 1)
            run(row_squares, i + 2, 2)
            if i == 0:
                quantise_weights()
            run(quantise, i + 0)
            run(project, i + 0)
            run(row_squares_on_vector, i + 2)
            run(store_k, i - 2)
            run(store_q, i - 1)
            run(regroup, i + 1, 0)
            run(invert_row_rms, i + 2)
            run(regroup, i + 1, 1)
